import numpy as np
import ml_dtypes


def mxq(x, axis, fmt="e4m3"):
    dtype, down = {"e4m3": (ml_dtypes.float8_e4m3fn, 7), "e5m2": (ml_dtypes.float8_e5m2, 14)}[fmt]
    v = np.moveaxis(np.asarray(x, np.float32).astype(ml_dtypes.bfloat16).astype(np.float64), axis, -1)
    blocks = v.reshape(v.shape[:-1] + (-1, 32))
    amax = np.abs(blocks).max(-1, keepdims=True)
    byte = np.maximum(np.where(amax > 0, np.frexp(amax)[1] - 1 + 127, 0) - down, 1)
    scale = np.exp2(byte - 127.0)
    codes = (blocks / scale).astype(np.float32).astype(dtype).astype(np.float64)
    return np.moveaxis((codes * scale).reshape(v.shape), -1, axis)


WIDE = False


def mx_kscale(k):
    if not WIDE:
        return np.ones(k)
    levels = np.array([10, -10, 5, -5, 0])
    a = np.random.permutation(np.resize(levels, k // 512 * 4)).reshape(k // 512, 4)
    idx = np.arange(k)
    return np.exp2(a[idx // 512, idx % 128 // 32])


BF16 = ml_dtypes.bfloat16


def bf(x):
    return np.asarray(x, np.float32).astype(BF16)


def f64(x):
    return np.asarray(x).astype(np.float64)


B, HH, WW, C, NH, KD, WS, SS = 4, 64, 64, 128, 8, 64, 8, 4
GH, GW, T, F = HH // WS, WW // WS, WS * WS, NH * KD
N = B * GH * GW


def setup_inputs():
    s = mx_kscale(F).reshape(NH, KD)
    return {"attn_ctx": bf(np.random.standard_normal((N, T, NH, KD)) * 0.4 * s),
            "x": bf(np.random.standard_normal((B, HH, WW, C))),
            "wo": bf(np.random.standard_normal((NH, KD, C)) * 2.0 / np.sqrt(F) / s[:, :, None]),
            "bo": bf(np.random.standard_normal(C) * 0.3)}


def reference(attn_ctx, x, wo, bo):
    o = f64(attn_ctx).reshape(N * T, F)
    proj = (mxq(o, 1, "e4m3") @ mxq(f64(wo).reshape(F, C), 0, "e4m3")) + f64(bo)
    merged = proj.reshape(B, GH, GW, WS, WS, C).swapaxes(2, 3).reshape(B, HH, WW, C)
    merged = np.roll(merged, shift=(SS, SS), axis=(1, 2))
    return f64(x) + merged

@@ -1,0 +1,208 @@
+from contextlib import ExitStack
+
+import concourse.mybir as mybir
+from concourse.masks import make_identity
+
+F32 = mybir.dt.float32
+BF16 = mybir.dt.bfloat16
+U32 = mybir.dt.uint32
+U8 = mybir.dt.uint8
+FP8X4 = mybir.dt.float8_e4m3fn_x4
+ADD = mybir.AluOpType.add
+
+P = 128
+FLOPS = 2 * 16384 * 512 * 128
+
+N_CHUNKS = 16
+N_UNITS = 2 * N_CHUNKS
+ATTN_BUFS = 6
+OUT_BUFS = 8
+X_CUTS = ((0, 12), (12, 36), (36, 64))
+GPSIMD_BIAS_UNITS = ()
+
+
+def tile_windowattentionblock_pb_t_kernel(tc, attn_ctx, x, wo, bo, out):
+    nc = tc.nc
+    attn_v = attn_ctx.rearrange(
+        "(bh bg gj) (ti tj) h d -> bh gj bg ti (tj h d)", bh=2, bg=16, gj=8, ti=8, tj=8
+    )
+    x_v = x.rearrange("(bh bl) i j c -> bh (bl i) j c", bh=2)
+    out_v = out.rearrange("(bh bl) i j c -> bh (bl i) j c", bh=2)
+    wo_v = wo.rearrange("h d c -> (h d) c").rearrange("(u q e) c -> q u (e c)", u=2, e=2)
+
+    with ExitStack() as ctx:
+        const = ctx.enter_context(tc.tile_pool(name="const", bufs=1))
+        attn_pool = ctx.enter_context(tc.tile_pool(name="attn", bufs=ATTN_BUFS))
+        grp_pool = ctx.enter_context(tc.tile_pool(name="grp", bufs=3))
+        code_pool = ctx.enter_context(tc.tile_pool(name="code", bufs=3))
+        out_pool = ctx.enter_context(tc.tile_pool(name="outp", bufs=OUT_BUFS))
+        tp_pool = ctx.enter_context(tc.psum_pool(name="tp", bufs=4))
+        mx_pool = ctx.enter_context(tc.psum_pool(name="mx", bufs=4))
+        ctx.enter_context(tc.manual_schedule())
+
+        attn_tiles = {}
+        x_tiles = {}
+        state = {}
+
+        def load_attn(c, pieces=1):
+            a_sb = attn_pool.tile([P, 4096], BF16, name="a_sb")
+            w = 4096 // pieces
+            for i in range(pieces):
+                nc.sync.dma_start(
+                    out=a_sb[:, i * w : (i + 1) * w],
+                    in_=attn_v[c // 8, c % 8][:, :, i * w : (i + 1) * w],
+                )
+                if c == 0 and i == 0:
+                    nc.sync.dma_start(
+                        out=w_raw[:].rearrange("p (u e) c -> p u (e c)", u=2), in_=wo_v
+                    )
+                    nc.sync.dma_start(out=brow[0:1, 0:P], in_=bo.unsqueeze(0))
+            attn_tiles[c] = a_sb
+
+        def load_x(bh, cut):
+            lo, hi = X_CUTS[cut]
+            nc.sync.dma_start(out=x_tiles[bh][:, lo:hi, :], in_=x_v[bh][:, lo:hi, :])
+
+        brow = const.tile([P, 256], BF16, name="brow")
+        ones = const.tile([P, P], BF16, name="ones")
+        nc.vector.memset(brow[:], 0.0)
+        nc.vector.memset(ones[:], 1.0)
+        ident = const.tile([P, P], F32, name="ident")
+        make_identity(nc, ident[:])
+        for bh in range(2):
+            x_tiles[bh] = const.tile([P, 64, P], BF16, name="x_sb%d" % bh)
+
+        w_raw = const.tile([P, 4, P], BF16, name="w_raw")
+        load_attn(0, pieces=2)
+        load_x(0, 0)
+        load_attn(1)
+        load_x(0, 1)
+        load_attn(2)
+        load_attn(3)
+        load_x(0, 2)
+        load_attn(4)
+        load_attn(5)
+
+        perm = const.tile([P, P], F32, name="perm")
+        for bl in range(2):
+            b0 = bl * 64
+            nc.vector.tensor_copy(out=perm[:, b0 + 4 : b0 + 64], in_=ident[:, b0 : b0 + 60])
+            nc.vector.tensor_copy(out=perm[:, b0 : b0 + 4], in_=ident[:, b0 + 60 : b0 + 64])
+
+        bias_bc = const.tile([P, P], F32, name="bias_bc")
+
+        def spread_bias():
+            bias_ps = mx_pool.tile([P, 4, P], F32, name="bias_ps", tag="mx")
+            nc.tensor.matmul(
+                out=bias_ps[:, 0:2, :].rearrange("p a c -> p (a c)"),
+                lhsT=ones[:],
+                rhs=brow[:],
+                start=True,
+                stop=True,
+            )
+            nc.vector.tensor_copy(out=bias_bc[:], in_=bias_ps[:, 0, :])
+
+        w_grp = const.tile([P, P, 4], BF16, name="w_grp", align_bytes=64)
+        nc.vector.tensor_copy(out=w_grp[:], in_=w_raw[:].rearrange("p t c -> p c t"))
+        w_codes = const.tile([P, P], U32, name="w_codes", align_bytes=64)
+        w_scales = const.tile([P, P], U8, name="w_scales", align_bytes=64)
+        nc.vector.quantize_mx(
+            out=w_codes[:].bitcast(FP8X4),
+            scales=w_scales[:],
+            in_=w_grp[:].rearrange("p c t -> p (c t)"),
+        )
+
+        def transpose_and_exit(u):
+            a32 = attn_tiles[u // 2][:].bitcast(F32)
+            grp = grp_pool.tile([P, 2048], BF16, name="grp", align_bytes=64)
+            g32 = grp[:].bitcast(F32)
+            banks = []
+            for b in range(2):
+                tp = tp_pool.tile([P, 2, 2, P], F32, name="tp")
+                for a in range(2):
+                    tj = (u % 2) * 4 + b * 2 + a
+                    for h in range(2):
+                        lo = tj * 256 + h * P
+                        nc.tensor.transpose(tp[:, a, h, :], a32[:, lo : lo + P], perm[:])
+                banks.append(tp)
+            for b in range(2):
+                nc.scalar.copy(
+                    out=g32[:, b * 512 : (b + 1) * 512].rearrange("p (a m h) -> p a m h", a=2, h=2),
+                    in_=banks[b][:].rearrange("p a h m -> p a m h"),
+                )
+            state[("grp", u)] = grp
+
+        def quantise(u):
+            codes = code_pool.tile([P, 512], U32, name="codes", align_bytes=64)
+            scales = code_pool.tile([P, 512], U8, name="scales", align_bytes=64)
+            nc.vector.quantize_mx(
+                out=codes[:].bitcast(FP8X4), scales=scales[:], in_=state[("grp", u)][:]
+            )
+            state[("codes", u)] = (codes, scales)
+
+        def multiply(u):
+            codes, scales = state[("codes", u)]
+            mx = mx_pool.tile([P, 4, P], F32, name="mx")
+            for a in range(4):
+                cols = slice(a * P, (a + 1) * P)
+                nc.tensor.matmul_mx(
+                    out=mx[:, a, :],
+                    lhsT=codes[:, cols].bitcast(FP8X4),
+                    lhsT_scale=scales[:, cols],
+                    rhs=w_codes[:].bitcast(FP8X4),
+                    rhs_scale=w_scales[:],
+                    start=True,
+                    stop=True,
+                )
+            state[("mx", u)] = mx
+
+        def add_bias(u):
+            c, half = u // 2, u % 2
+            if half == 0:
+                state[("o", c)] = out_pool.tile([P, 8, P], F32, name="o_sb")
+            o_sb = state[("o", c)]
+            px = ((c % 8) * 8 + 4 + half * 4) % 64
+            eng = nc.gpsimd if u in GPSIMD_BIAS_UNITS else nc.vector
+            eng.tensor_tensor(
+                out=o_sb[:, half * 4 : half * 4 + 4, :],
+                in0=x_tiles[c // 8][:, px : px + 4, :],
+                in1=bias_bc[:].unsqueeze(1).to_broadcast([P, 4, P]),
+                op=ADD,
+            )
+
+        def add_product(u):
+            c, half = u // 2, u % 2
+            o_half = state[("o", c)][:, half * 4 : half * 4 + 4, :]
+            nc.vector.tensor_tensor(out=o_half, in0=state[("mx", u)][:], in1=o_half, op=ADD)
+
+        def store(c):
+            bh, gj = c // 8, c % 8
+            o_sb = state[("o", c)]
+            if gj < 7:
+                nc.sync.dma_start(out=out_v[bh][:, gj * 8 + 4 : gj * 8 + 12, :], in_=o_sb[:])
+            else:
+                nc.sync.dma_start(out=out_v[bh][:, 60:64, :], in_=o_sb[:, 0:4, :])
+                nc.sync.dma_start(out=out_v[bh][:, 0:4, :], in_=o_sb[:, 4:8, :])
+
+        late_x = {7: (1, 0), 8: (1, 1), 10: (1, 2)}
+
+        for s in range(N_UNITS + 3):
+            if s < N_UNITS:
+                transpose_and_exit(s)
+            if 0 <= s - 1 < N_UNITS:
+                quantise(s - 1)
+                if s == 1:
+                    spread_bias()
+                add_bias(s - 1)
+            if 0 <= s - 2 < N_UNITS:
+                multiply(s - 2)
+            if s < N_UNITS and s % 2 == 1:
+                c_next = s // 2 + ATTN_BUFS
+                if c_next < N_CHUNKS:
+                    load_attn(c_next)
+                    if c_next in late_x:
+                        load_x(late_x[c_next][0], late_x[c_next][1])
+            if 0 <= s - 3 < N_UNITS:
+                add_product(s - 3)
+                if (s - 3) % 2 == 1:
+                    store((s - 3) // 2)

@@ -19,6 +19,7 @@ ATTN_BUFS = 6
 OUT_BUFS = 8
 X_CUTS = ((0, 12), (12, 36), (36, 64))
 GPSIMD_BIAS_UNITS = ()
+N_DUMMY = 2
 
 
 def tile_windowattentionblock_pb_t_kernel(tc, attn_ctx, x, wo, bo, out):
@@ -37,9 +38,11 @@ def tile_windowattentionblock_pb_t_kernel(tc, attn_ctx, x, wo, bo, out):
         code_pool = ctx.enter_context(tc.tile_pool(name="code", bufs=3))
         out_pool = ctx.enter_context(tc.tile_pool(name="outp", bufs=OUT_BUFS))
         tp_pool = ctx.enter_context(tc.psum_pool(name="tp", bufs=4))
-        mx_pool = ctx.enter_context(tc.psum_pool(name="mx", bufs=4))
+        mx_pool = ctx.enter_context(tc.psum_pool(name="mx", bufs=3))
+        scr_pool = ctx.enter_context(tc.psum_pool(name="scr", bufs=1))
         ctx.enter_context(tc.manual_schedule())
 
+        scratch = scr_pool.tile([P, 512], F32, name="scratch")
         attn_tiles = {}
         x_tiles = {}
         state = {}
@@ -151,6 +154,16 @@ def tile_windowattentionblock_pb_t_kernel(tc, attn_ctx, x, wo, bo, out):
                     lhsT_scale=scales[:, cols],
                     rhs=w_codes[:].bitcast(FP8X4),
                     rhs_scale=w_scales[:],
+                    start=True,
+                    stop=True,
+                )
+            for i in range(N_DUMMY):
+                nc.tensor.matmul_mx(
+                    out=scratch[:],
+                    lhsT=w_codes[:].bitcast(FP8X4),
+                    lhsT_scale=w_scales[:],
+                    rhs=codes[:].bitcast(FP8X4),
+                    rhs_scale=scales[:],
                     start=True,
                     stop=True,
                 )

@@ -17,18 +17,14 @@ N_CHUNKS = 16
 N_UNITS = 2 * N_CHUNKS
 ATTN_BUFS = 6
 OUT_BUFS = 8
-X_CUTS = ((0, 12), (12, 36), (36, 64))
 GPSIMD_BIAS_UNITS = ()
-N_DUMMY = 2
 
 
 def tile_windowattentionblock_pb_t_kernel(tc, attn_ctx, x, wo, bo, out):
     nc = tc.nc
-    attn_v = attn_ctx.rearrange(
-        "(bh bg gj) (ti tj) h d -> bh gj bg ti (tj h d)", bh=2, bg=16, gj=8, ti=8, tj=8
-    )
-    x_v = x.rearrange("(bh bl) i j c -> bh (bl i) j c", bh=2)
-    out_v = out.rearrange("(bh bl) i j c -> bh (bl i) j c", bh=2)
+    attn_v = attn_ctx.rearrange("n (ti tj) h d -> (n ti) (tj h d)", tj=8)
+    x_v = x.rearrange("b i (s r) c -> (b i s) (r c)", r=8)
+    out_v = out.rearrange("b i (s r) c -> (b i s) (r c)", r=8)
     wo_v = wo.rearrange("h d c -> (h d) c").rearrange("(u q e) c -> q u (e c)", u=2, e=2)
 
     with ExitStack() as ctx:
@@ -38,14 +34,30 @@ def tile_windowattentionblock_pb_t_kernel(tc, attn_ctx, x, wo, bo, out):
         code_pool = ctx.enter_context(tc.tile_pool(name="code", bufs=3))
         out_pool = ctx.enter_context(tc.tile_pool(name="outp", bufs=OUT_BUFS))
         tp_pool = ctx.enter_context(tc.psum_pool(name="tp", bufs=4))
-        mx_pool = ctx.enter_context(tc.psum_pool(name="mx", bufs=3))
-        scr_pool = ctx.enter_context(tc.psum_pool(name="scr", bufs=1))
+        mx_pool = ctx.enter_context(tc.psum_pool(name="mx", bufs=4))
         ctx.enter_context(tc.manual_schedule())
 
-        scratch = scr_pool.tile([P, 512], F32, name="scratch")
         attn_tiles = {}
         x_tiles = {}
         state = {}
+
+        def slot_ranges(c):
+            b, a = c // 4, c % 4
+            if a < 3:
+                return [(0, P, (b * 64 + 16 * a + 4) * 8)]
+            return [(0, 96, (b * 64 + 52) * 8), (96, 32, b * 64 * 8)]
+
+        def load_x(b, wrap):
+            x_sb = x_tiles[b]
+            if not wrap:
+                s0 = (b * 64 + 4) * 8
+                nc.sync.dma_start(
+                    out=x_sb[:, 0:3, :],
+                    in_=x_v[s0 : s0 + 3 * P, :].rearrange("(t q) f -> q t f", q=P),
+                )
+            else:
+                for p0, n, s0 in slot_ranges(b * 4 + 3):
+                    nc.sync.dma_start(out=x_sb[p0 : p0 + n, 3, :], in_=x_v[s0 : s0 + n, :])
 
         def load_attn(c, pieces=1):
             a_sb = attn_pool.tile([P, 4096], BF16, name="a_sb")
@@ -53,7 +65,7 @@ def tile_windowattentionblock_pb_t_kernel(tc, attn_ctx, x, wo, bo, out):
             for i in range(pieces):
                 nc.sync.dma_start(
                     out=a_sb[:, i * w : (i + 1) * w],
-                    in_=attn_v[c // 8, c % 8][:, :, i * w : (i + 1) * w],
+                    in_=attn_v[c * P : (c + 1) * P, i * w : (i + 1) * w],
                 )
                 if c == 0 and i == 0:
                     nc.sync.dma_start(
@@ -62,9 +74,12 @@ def tile_windowattentionblock_pb_t_kernel(tc, attn_ctx, x, wo, bo, out):
                     nc.sync.dma_start(out=brow[0:1, 0:P], in_=bo.unsqueeze(0))
             attn_tiles[c] = a_sb
 
-        def load_x(bh, cut):
-            lo, hi = X_CUTS[cut]
-            nc.sync.dma_start(out=x_tiles[bh][:, lo:hi, :], in_=x_v[bh][:, lo:hi, :])
+        def load_chunk(c):
+            if c > 0 and c % 4 == 0:
+                load_x(c // 4, False)
+            if c % 4 == 3:
+                load_x(c // 4, True)
+            load_attn(c)
 
         brow = const.tile([P, 256], BF16, name="brow")
         ones = const.tile([P, P], BF16, name="ones")
@@ -72,25 +87,25 @@ def tile_windowattentionblock_pb_t_kernel(tc, attn_ctx, x, wo, bo, out):
         nc.vector.memset(ones[:], 1.0)
         ident = const.tile([P, P], F32, name="ident")
         make_identity(nc, ident[:])
-        for bh in range(2):
-            x_tiles[bh] = const.tile([P, 64, P], BF16, name="x_sb%d" % bh)
+        for b in range(4):
+            x_tiles[b] = const.tile([P, 4, 1024], BF16, name="x_sb%d" % b)
 
         w_raw = const.tile([P, 4, P], BF16, name="w_raw")
         load_attn(0, pieces=2)
-        load_x(0, 0)
-        load_attn(1)
-        load_x(0, 1)
-        load_attn(2)
-        load_attn(3)
-        load_x(0, 2)
-        load_attn(4)
-        load_attn(5)
+        load_x(0, False)
+        for c in range(1, ATTN_BUFS):
+            load_chunk(c)
 
-        perm = const.tile([P, P], F32, name="perm")
-        for bl in range(2):
-            b0 = bl * 64
-            nc.vector.tensor_copy(out=perm[:, b0 + 4 : b0 + 64], in_=ident[:, b0 : b0 + 60])
-            nc.vector.tensor_copy(out=perm[:, b0 : b0 + 4], in_=ident[:, b0 + 60 : b0 + 64])
+        id_v = ident[:].rearrange("p (g j t) -> p g t j", g=2, j=8)
+        perm_a = const.tile([P, 2, 8, 8], F32, name="perm_a")
+        perm_b = const.tile([P, 2, 8, 8], F32, name="perm_b")
+        nc.vector.tensor_copy(out=perm_a[:], in_=id_v)
+        nc.vector.tensor_copy(out=perm_b[:, :, :, 1:8], in_=id_v[:, :, :, 0:7])
+        nc.vector.tensor_copy(out=perm_b[:, :, :, 0:1], in_=id_v[:, :, :, 7:8])
+        perms = [
+            perm_a[:].rearrange("p g t s -> p (g t s)"),
+            perm_b[:].rearrange("p g t s -> p (g t s)"),
+        ]
 
         bias_bc = const.tile([P, P], F32, name="bias_bc")
 
@@ -126,7 +141,7 @@ def tile_windowattentionblock_pb_t_kernel(tc, attn_ctx, x, wo, bo, out):
                     tj = (u % 2) * 4 + b * 2 + a
                     for h in range(2):
                         lo = tj * 256 + h * P
-                        nc.tensor.transpose(tp[:, a, h, :], a32[:, lo : lo + P], perm[:])
+                        nc.tensor.transpose(tp[:, a, h, :], a32[:, lo : lo + P], perms[u % 2])
                 banks.append(tp)
             for b in range(2):
                 nc.scalar.copy(
@@ -157,47 +172,37 @@ def tile_windowattentionblock_pb_t_kernel(tc, attn_ctx, x, wo, bo, out):
                     start=True,
                     stop=True,
                 )
-            for i in range(N_DUMMY):
-                nc.tensor.matmul_mx(
-                    out=scratch[:],
-                    lhsT=w_codes[:].bitcast(FP8X4),
-                    lhsT_scale=w_scales[:],
-                    rhs=codes[:].bitcast(FP8X4),
-                    rhs_scale=scales[:],
-                    start=True,
-                    stop=True,
-                )
             state[("mx", u)] = mx
 
+        def o_half(u):
+            lo = 512 if u % 2 == 0 else 0
+            return slice(lo, lo + 512)
+
         def add_bias(u):
-            c, half = u // 2, u % 2
-            if half == 0:
-                state[("o", c)] = out_pool.tile([P, 8, P], F32, name="o_sb")
-            o_sb = state[("o", c)]
-            px = ((c % 8) * 8 + 4 + half * 4) % 64
+            c = u // 2
+            if u % 2 == 0:
+                state[("o", c)] = out_pool.tile([P, 1024], F32, name="o_sb")
             eng = nc.gpsimd if u in GPSIMD_BIAS_UNITS else nc.vector
             eng.tensor_tensor(
-                out=o_sb[:, half * 4 : half * 4 + 4, :],
-                in0=x_tiles[c // 8][:, px : px + 4, :],
+                out=state[("o", c)][:, o_half(u)].rearrange("p (r c) -> p r c", r=4),
+                in0=x_tiles[c // 4][:, c % 4, o_half(u)].rearrange("p (r c) -> p r c", r=4),
                 in1=bias_bc[:].unsqueeze(1).to_broadcast([P, 4, P]),
                 op=ADD,
             )
 
         def add_product(u):
-            c, half = u // 2, u % 2
-            o_half = state[("o", c)][:, half * 4 : half * 4 + 4, :]
-            nc.vector.tensor_tensor(out=o_half, in0=state[("mx", u)][:], in1=o_half, op=ADD)
+            o_part = state[("o", u // 2)][:, o_half(u)]
+            nc.vector.tensor_tensor(
+                out=o_part,
+                in0=state[("mx", u)][:].rearrange("p a c -> p (a c)"),
+                in1=o_part,
+                op=ADD,
+            )
 
         def store(c):
-            bh, gj = c // 8, c % 8
             o_sb = state[("o", c)]
-            if gj < 7:
-                nc.sync.dma_start(out=out_v[bh][:, gj * 8 + 4 : gj * 8 + 12, :], in_=o_sb[:])
-            else:
-                nc.sync.dma_start(out=out_v[bh][:, 60:64, :], in_=o_sb[:, 0:4, :])
-                nc.sync.dma_start(out=out_v[bh][:, 0:4, :], in_=o_sb[:, 4:8, :])
-
-        late_x = {7: (1, 0), 8: (1, 1), 10: (1, 2)}
+            for p0, n, s0 in slot_ranges(c):
+                nc.sync.dma_start(out=out_v[s0 : s0 + n, :], in_=o_sb[p0 : p0 + n, :])
 
         for s in range(N_UNITS + 3):
             if s < N_UNITS:
@@ -212,9 +217,7 @@ def tile_windowattentionblock_pb_t_kernel(tc, attn_ctx, x, wo, bo, out):
             if s < N_UNITS and s % 2 == 1:
                 c_next = s // 2 + ATTN_BUFS
                 if c_next < N_CHUNKS:
-                    load_attn(c_next)
-                    if c_next in late_x:
-                        load_x(late_x[c_next][0], late_x[c_next][1])
+                    load_chunk(c_next)
             if 0 <= s - 3 < N_UNITS:
                 add_product(s - 3)
                 if (s - 3) % 2 == 1:

@@ -17,7 +17,7 @@ N_CHUNKS = 16
 N_UNITS = 2 * N_CHUNKS
 ATTN_BUFS = 6
 OUT_BUFS = 8
-GPSIMD_BIAS_UNITS = ()
+GPSIMD_BIAS_UNITS = tuple(range(N_UNITS))
 
 
 def tile_windowattentionblock_pb_t_kernel(tc, attn_ctx, x, wo, bo, out):

@@ -17,7 +17,7 @@ N_CHUNKS = 16
 N_UNITS = 2 * N_CHUNKS
 ATTN_BUFS = 6
 OUT_BUFS = 8
-GPSIMD_BIAS_UNITS = tuple(range(N_UNITS))
+OWN = 96
 
 
 def tile_windowattentionblock_pb_t_kernel(tc, attn_ctx, x, wo, bo, out):
@@ -30,8 +30,9 @@ def tile_windowattentionblock_pb_t_kernel(tc, attn_ctx, x, wo, bo, out):
     with ExitStack() as ctx:
         const = ctx.enter_context(tc.tile_pool(name="const", bufs=1))
         attn_pool = ctx.enter_context(tc.tile_pool(name="attn", bufs=ATTN_BUFS))
-        grp_pool = ctx.enter_context(tc.tile_pool(name="grp", bufs=3))
-        code_pool = ctx.enter_context(tc.tile_pool(name="code", bufs=3))
+        grp_pool = ctx.enter_context(tc.tile_pool(name="grp", bufs=6))
+        grp0_pool = ctx.enter_context(tc.tile_pool(name="grp0", bufs=4))
+        code_pool = ctx.enter_context(tc.tile_pool(name="code", bufs=5))
         out_pool = ctx.enter_context(tc.tile_pool(name="outp", bufs=OUT_BUFS))
         tp_pool = ctx.enter_context(tc.psum_pool(name="tp", bufs=4))
         mx_pool = ctx.enter_context(tc.psum_pool(name="mx", bufs=4))
@@ -41,23 +42,11 @@ def tile_windowattentionblock_pb_t_kernel(tc, attn_ctx, x, wo, bo, out):
         x_tiles = {}
         state = {}
 
-        def slot_ranges(c):
-            b, a = c // 4, c % 4
-            if a < 3:
-                return [(0, P, (b * 64 + 16 * a + 4) * 8)]
-            return [(0, 96, (b * 64 + 52) * 8), (96, 32, b * 64 * 8)]
-
-        def load_x(b, wrap):
-            x_sb = x_tiles[b]
-            if not wrap:
-                s0 = (b * 64 + 4) * 8
-                nc.sync.dma_start(
-                    out=x_sb[:, 0:3, :],
-                    in_=x_v[s0 : s0 + 3 * P, :].rearrange("(t q) f -> q t f", q=P),
-                )
-            else:
-                for p0, n, s0 in slot_ranges(b * 4 + 3):
-                    nc.sync.dma_start(out=x_sb[p0 : p0 + n, 3, :], in_=x_v[s0 : s0 + n, :])
+        def load_x(b):
+            nc.sync.dma_start(
+                out=x_tiles[b][:],
+                in_=x_v[b * 4 * P : (b + 1) * 4 * P, :].rearrange("(t q) f -> q t f", q=P),
+            )
 
         def load_attn(c, pieces=1):
             a_sb = attn_pool.tile([P, 4096], BF16, name="a_sb")
@@ -75,10 +64,8 @@ def tile_windowattentionblock_pb_t_kernel(tc, attn_ctx, x, wo, bo, out):
             attn_tiles[c] = a_sb
 
         def load_chunk(c):
-            if c > 0 and c % 4 == 0:
-                load_x(c // 4, False)
-            if c % 4 == 3:
-                load_x(c // 4, True)
+            if c % 4 == 1:
+                load_x(c // 4)
             load_attn(c)
 
         brow = const.tile([P, 256], BF16, name="brow")
@@ -92,7 +79,6 @@ def tile_windowattentionblock_pb_t_kernel(tc, attn_ctx, x, wo, bo, out):
 
         w_raw = const.tile([P, 4, P], BF16, name="w_raw")
         load_attn(0, pieces=2)
-        load_x(0, False)
         for c in range(1, ATTN_BUFS):
             load_chunk(c)
 
@@ -130,36 +116,45 @@ def tile_windowattentionblock_pb_t_kernel(tc, attn_ctx, x, wo, bo, out):
             in_=w_grp[:].rearrange("p c t -> p (c t)"),
         )
 
+        def grp_of(t, half):
+            key = ("grp", t, half)
+            if key not in state:
+                if t % 4 == 0:
+                    state[key] = grp0_pool.tile([P, 2048], BF16, name="grp0", align_bytes=64)
+                else:
+                    state[key] = grp_pool.tile([P, 2048], BF16, name="grp", align_bytes=64)
+            return state[key]
+
         def transpose_and_exit(u):
-            a32 = attn_tiles[u // 2][:].bitcast(F32)
-            grp = grp_pool.tile([P, 2048], BF16, name="grp", align_bytes=64)
-            g32 = grp[:].bitcast(F32)
+            c, half = u // 2, u % 2
+            a32 = attn_tiles[c][:].bitcast(F32)
+            t_next = (c // 4) * 4 + (c + 1) % 4
+            own32 = grp_of(c, half)[:].bitcast(F32).rearrange("p (j m h) -> p j m h", j=4, h=2)
+            next32 = grp_of(t_next, half)[:].bitcast(F32).rearrange("p (j m h) -> p j m h", j=4, h=2)
             banks = []
             for b in range(2):
                 tp = tp_pool.tile([P, 2, 2, P], F32, name="tp")
                 for a in range(2):
-                    tj = (u % 2) * 4 + b * 2 + a
+                    tj = half * 4 + b * 2 + a
                     for h in range(2):
                         lo = tj * 256 + h * P
-                        nc.tensor.transpose(tp[:, a, h, :], a32[:, lo : lo + P], perms[u % 2])
+                        nc.tensor.transpose(tp[:, a, h, :], a32[:, lo : lo + P], perms[half])
                 banks.append(tp)
             for b in range(2):
-                nc.scalar.copy(
-                    out=g32[:, b * 512 : (b + 1) * 512].rearrange("p (a m h) -> p a m h", a=2, h=2),
-                    in_=banks[b][:].rearrange("p a h m -> p a m h"),
-                )
-            state[("grp", u)] = grp
+                src = banks[b][:].rearrange("p a h m -> p a m h")
+                nc.scalar.copy(out=own32[:, 2 * b : 2 * b + 2, P - OWN : P, :], in_=src[:, :, 0:OWN, :])
+                nc.scalar.copy(out=next32[:, 2 * b : 2 * b + 2, 0 : P - OWN, :], in_=src[:, :, OWN:P, :])
 
-        def quantise(u):
+        def quantise(t, half):
             codes = code_pool.tile([P, 512], U32, name="codes", align_bytes=64)
             scales = code_pool.tile([P, 512], U8, name="scales", align_bytes=64)
             nc.vector.quantize_mx(
-                out=codes[:].bitcast(FP8X4), scales=scales[:], in_=state[("grp", u)][:]
+                out=codes[:].bitcast(FP8X4), scales=scales[:], in_=state[("grp", t, half)][:]
             )
-            state[("codes", u)] = (codes, scales)
+            state[("codes", t, half)] = (codes, scales)
 
-        def multiply(u):
-            codes, scales = state[("codes", u)]
+        def multiply(t, half):
+            codes, scales = state[("codes", t, half)]
             mx = mx_pool.tile([P, 4, P], F32, name="mx")
             for a in range(4):
                 cols = slice(a * P, (a + 1) * P)
@@ -172,53 +167,60 @@ def tile_windowattentionblock_pb_t_kernel(tc, attn_ctx, x, wo, bo, out):
                     start=True,
                     stop=True,
                 )
-            state[("mx", u)] = mx
+            state[("mx", t, half)] = mx
 
-        def o_half(u):
-            lo = 512 if u % 2 == 0 else 0
+        def o_half(half):
+            lo = 512 if half == 0 else 0
             return slice(lo, lo + 512)
 
-        def add_bias(u):
-            c = u // 2
-            if u % 2 == 0:
-                state[("o", c)] = out_pool.tile([P, 1024], F32, name="o_sb")
-            eng = nc.gpsimd if u in GPSIMD_BIAS_UNITS else nc.vector
-            eng.tensor_tensor(
-                out=state[("o", c)][:, o_half(u)].rearrange("p (r c) -> p r c", r=4),
-                in0=x_tiles[c // 4][:, c % 4, o_half(u)].rearrange("p (r c) -> p r c", r=4),
+        def add_bias(t, half):
+            if half == 0:
+                state[("o", t)] = out_pool.tile([P, 1024], F32, name="o_sb")
+            nc.vector.tensor_tensor(
+                out=state[("o", t)][:, o_half(half)].rearrange("p (r c) -> p r c", r=4),
+                in0=x_tiles[t // 4][:, t % 4, o_half(half)].rearrange("p (r c) -> p r c", r=4),
                 in1=bias_bc[:].unsqueeze(1).to_broadcast([P, 4, P]),
                 op=ADD,
             )
 
-        def add_product(u):
-            o_part = state[("o", u // 2)][:, o_half(u)]
+        def add_product(t, half):
+            o_part = state[("o", t)][:, o_half(half)]
             nc.vector.tensor_tensor(
                 out=o_part,
-                in0=state[("mx", u)][:].rearrange("p a c -> p (a c)"),
+                in0=state[("mx", t, half)][:].rearrange("p a c -> p (a c)"),
                 in1=o_part,
                 op=ADD,
             )
+            if half == 1:
+                nc.sync.dma_start(out=out_v[t * P : (t + 1) * P, :], in_=state[("o", t)][:])
 
-        def store(c):
-            o_sb = state[("o", c)]
-            for p0, n, s0 in slot_ranges(c):
-                nc.sync.dma_start(out=out_v[s0 : s0 + n, :], in_=o_sb[p0 : p0 + n, :])
+        def complete_after(u):
+            c, half = u // 2, u % 2
+            done = []
+            if c % 4 != 0:
+                done.append((c, half))
+            elif c > 0:
+                done.append((c - 4, half))
+            if c == N_CHUNKS - 1:
+                done.append((c - 3, half))
+            return done
 
         for s in range(N_UNITS + 3):
             if s < N_UNITS:
                 transpose_and_exit(s)
+            if s == 1:
+                spread_bias()
             if 0 <= s - 1 < N_UNITS:
-                quantise(s - 1)
-                if s == 1:
-                    spread_bias()
-                add_bias(s - 1)
+                for t, half in complete_after(s - 1):
+                    quantise(t, half)
+                    add_bias(t, half)
             if 0 <= s - 2 < N_UNITS:
-                multiply(s - 2)
+                for t, half in complete_after(s - 2):
+                    multiply(t, half)
             if s < N_UNITS and s % 2 == 1:
                 c_next = s // 2 + ATTN_BUFS
                 if c_next < N_CHUNKS:
                     load_chunk(c_next)
             if 0 <= s - 3 < N_UNITS:
-                add_product(s - 3)
-                if (s - 3) % 2 == 1:
-                    store((s - 3) // 2)
+                for t, half in complete_after(s - 3):
+                    add_product(t, half)

@@ -17,7 +17,9 @@ N_CHUNKS = 16
 N_UNITS = 2 * N_CHUNKS
 ATTN_BUFS = 6
 OUT_BUFS = 8
-OWN = 96
+GPSIMD_BIAS_UNITS = ()
+N_DUMMY = 2
+LAG = 3
 
 
 def tile_windowattentionblock_pb_t_kernel(tc, attn_ctx, x, wo, bo, out):
@@ -30,23 +32,36 @@ def tile_windowattentionblock_pb_t_kernel(tc, attn_ctx, x, wo, bo, out):
     with ExitStack() as ctx:
         const = ctx.enter_context(tc.tile_pool(name="const", bufs=1))
         attn_pool = ctx.enter_context(tc.tile_pool(name="attn", bufs=ATTN_BUFS))
-        grp_pool = ctx.enter_context(tc.tile_pool(name="grp", bufs=6))
-        grp0_pool = ctx.enter_context(tc.tile_pool(name="grp0", bufs=4))
+        grp_pool = ctx.enter_context(tc.tile_pool(name="grp", bufs=3))
         code_pool = ctx.enter_context(tc.tile_pool(name="code", bufs=5))
         out_pool = ctx.enter_context(tc.tile_pool(name="outp", bufs=OUT_BUFS))
         tp_pool = ctx.enter_context(tc.psum_pool(name="tp", bufs=4))
-        mx_pool = ctx.enter_context(tc.psum_pool(name="mx", bufs=4))
+        mx_pool = ctx.enter_context(tc.psum_pool(name="mx", bufs=3))
+        scr_pool = ctx.enter_context(tc.psum_pool(name="scr", bufs=1))
         ctx.enter_context(tc.manual_schedule())
 
+        scratch = scr_pool.tile([P, 512], F32, name="scratch")
         attn_tiles = {}
         x_tiles = {}
         state = {}
 
-        def load_x(b):
-            nc.sync.dma_start(
-                out=x_tiles[b][:],
-                in_=x_v[b * 4 * P : (b + 1) * 4 * P, :].rearrange("(t q) f -> q t f", q=P),
-            )
+        def slot_ranges(c):
+            b, a = c // 4, c % 4
+            if a < 3:
+                return [(0, P, (b * 64 + 16 * a + 4) * 8)]
+            return [(0, 96, (b * 64 + 52) * 8), (96, 32, b * 64 * 8)]
+
+        def load_x(b, wrap):
+            x_sb = x_tiles[b]
+            if not wrap:
+                s0 = (b * 64 + 4) * 8
+                nc.sync.dma_start(
+                    out=x_sb[:, 0:3, :],
+                    in_=x_v[s0 : s0 + 3 * P, :].rearrange("(t q) f -> q t f", q=P),
+                )
+            else:
+                for p0, n, s0 in slot_ranges(b * 4 + 3):
+                    nc.sync.dma_start(out=x_sb[p0 : p0 + n, 3, :], in_=x_v[s0 : s0 + n, :])
 
         def load_attn(c, pieces=1):
             a_sb = attn_pool.tile([P, 4096], BF16, name="a_sb")
@@ -64,8 +79,10 @@ def tile_windowattentionblock_pb_t_kernel(tc, attn_ctx, x, wo, bo, out):
             attn_tiles[c] = a_sb
 
         def load_chunk(c):
-            if c % 4 == 1:
-                load_x(c // 4)
+            if c > 0 and c % 4 == 0:
+                load_x(c // 4, False)
+            if c % 4 == 3:
+                load_x(c // 4, True)
             load_attn(c)
 
         brow = const.tile([P, 256], BF16, name="brow")
@@ -79,6 +96,7 @@ def tile_windowattentionblock_pb_t_kernel(tc, attn_ctx, x, wo, bo, out):
 
         w_raw = const.tile([P, 4, P], BF16, name="w_raw")
         load_attn(0, pieces=2)
+        load_x(0, False)
         for c in range(1, ATTN_BUFS):
             load_chunk(c)
 
@@ -116,45 +134,36 @@ def tile_windowattentionblock_pb_t_kernel(tc, attn_ctx, x, wo, bo, out):
             in_=w_grp[:].rearrange("p c t -> p (c t)"),
         )
 
-        def grp_of(t, half):
-            key = ("grp", t, half)
-            if key not in state:
-                if t % 4 == 0:
-                    state[key] = grp0_pool.tile([P, 2048], BF16, name="grp0", align_bytes=64)
-                else:
-                    state[key] = grp_pool.tile([P, 2048], BF16, name="grp", align_bytes=64)
-            return state[key]
-
         def transpose_and_exit(u):
-            c, half = u // 2, u % 2
-            a32 = attn_tiles[c][:].bitcast(F32)
-            t_next = (c // 4) * 4 + (c + 1) % 4
-            own32 = grp_of(c, half)[:].bitcast(F32).rearrange("p (j m h) -> p j m h", j=4, h=2)
-            next32 = grp_of(t_next, half)[:].bitcast(F32).rearrange("p (j m h) -> p j m h", j=4, h=2)
+            a32 = attn_tiles[u // 2][:].bitcast(F32)
+            grp = grp_pool.tile([P, 2048], BF16, name="grp", align_bytes=64)
+            g32 = grp[:].bitcast(F32)
             banks = []
             for b in range(2):
                 tp = tp_pool.tile([P, 2, 2, P], F32, name="tp")
                 for a in range(2):
-                    tj = half * 4 + b * 2 + a
+                    tj = (u % 2) * 4 + b * 2 + a
                     for h in range(2):
                         lo = tj * 256 + h * P
-                        nc.tensor.transpose(tp[:, a, h, :], a32[:, lo : lo + P], perms[half])
+                        nc.tensor.transpose(tp[:, a, h, :], a32[:, lo : lo + P], perms[u % 2])
                 banks.append(tp)
             for b in range(2):
-                src = banks[b][:].rearrange("p a h m -> p a m h")
-                nc.scalar.copy(out=own32[:, 2 * b : 2 * b + 2, P - OWN : P, :], in_=src[:, :, 0:OWN, :])
-                nc.scalar.copy(out=next32[:, 2 * b : 2 * b + 2, 0 : P - OWN, :], in_=src[:, :, OWN:P, :])
+                nc.scalar.copy(
+                    out=g32[:, b * 512 : (b + 1) * 512].rearrange("p (a m h) -> p a m h", a=2, h=2),
+                    in_=banks[b][:].rearrange("p a h m -> p a m h"),
+                )
+            state[("grp", u)] = grp
 
-        def quantise(t, half):
+        def quantise(u):
             codes = code_pool.tile([P, 512], U32, name="codes", align_bytes=64)
             scales = code_pool.tile([P, 512], U8, name="scales", align_bytes=64)
             nc.vector.quantize_mx(
-                out=codes[:].bitcast(FP8X4), scales=scales[:], in_=state[("grp", t, half)][:]
+                out=codes[:].bitcast(FP8X4), scales=scales[:], in_=state[("grp", u)][:]
             )
-            state[("codes", t, half)] = (codes, scales)
+            state[("codes", u)] = (codes, scales)
 
-        def multiply(t, half):
-            codes, scales = state[("codes", t, half)]
+        def multiply(u):
+            codes, scales = state[("codes", u)]
             mx = mx_pool.tile([P, 4, P], F32, name="mx")
             for a in range(4):
                 cols = slice(a * P, (a + 1) * P)
@@ -167,60 +176,64 @@ def tile_windowattentionblock_pb_t_kernel(tc, attn_ctx, x, wo, bo, out):
                     start=True,
                     stop=True,
                 )
-            state[("mx", t, half)] = mx
+            if u < N_UNITS - 3:
+                for i in range(N_DUMMY):
+                    nc.tensor.matmul_mx(
+                        out=scratch[:],
+                        lhsT=w_codes[:].bitcast(FP8X4),
+                        lhsT_scale=w_scales[:],
+                        rhs=codes[:].bitcast(FP8X4),
+                        rhs_scale=scales[:],
+                        start=True,
+                        stop=True,
+                    )
+            state[("mx", u)] = mx
 
-        def o_half(half):
-            lo = 512 if half == 0 else 0
+        def o_half(u):
+            lo = 512 if u % 2 == 0 else 0
             return slice(lo, lo + 512)
 
-        def add_bias(t, half):
-            if half == 0:
-                state[("o", t)] = out_pool.tile([P, 1024], F32, name="o_sb")
-            nc.vector.tensor_tensor(
-                out=state[("o", t)][:, o_half(half)].rearrange("p (r c) -> p r c", r=4),
-                in0=x_tiles[t // 4][:, t % 4, o_half(half)].rearrange("p (r c) -> p r c", r=4),
+        def add_bias(u):
+            c = u // 2
+            if u % 2 == 0:
+                state[("o", c)] = out_pool.tile([P, 1024], F32, name="o_sb")
+            eng = nc.gpsimd if u in GPSIMD_BIAS_UNITS else nc.vector
+            eng.tensor_tensor(
+                out=state[("o", c)][:, o_half(u)].rearrange("p (r c) -> p r c", r=4),
+                in0=x_tiles[c // 4][:, c % 4, o_half(u)].rearrange("p (r c) -> p r c", r=4),
                 in1=bias_bc[:].unsqueeze(1).to_broadcast([P, 4, P]),
                 op=ADD,
             )
 
-        def add_product(t, half):
-            o_part = state[("o", t)][:, o_half(half)]
+        def add_product(u):
+            o_part = state[("o", u // 2)][:, o_half(u)]
             nc.vector.tensor_tensor(
                 out=o_part,
-                in0=state[("mx", t, half)][:].rearrange("p a c -> p (a c)"),
+                in0=state[("mx", u)][:].rearrange("p a c -> p (a c)"),
                 in1=o_part,
                 op=ADD,
             )
-            if half == 1:
-                nc.sync.dma_start(out=out_v[t * P : (t + 1) * P, :], in_=state[("o", t)][:])
 
-        def complete_after(u):
-            c, half = u // 2, u % 2
-            done = []
-            if c % 4 != 0:
-                done.append((c, half))
-            elif c > 0:
-                done.append((c - 4, half))
-            if c == N_CHUNKS - 1:
-                done.append((c - 3, half))
-            return done
+        def store(c):
+            o_sb = state[("o", c)]
+            for p0, n, s0 in slot_ranges(c):
+                nc.sync.dma_start(out=out_v[s0 : s0 + n, :], in_=o_sb[p0 : p0 + n, :])
 
-        for s in range(N_UNITS + 3):
+        for s in range(N_UNITS + LAG + 1):
             if s < N_UNITS:
                 transpose_and_exit(s)
-            if s == 1:
-                spread_bias()
             if 0 <= s - 1 < N_UNITS:
-                for t, half in complete_after(s - 1):
-                    quantise(t, half)
-                    add_bias(t, half)
-            if 0 <= s - 2 < N_UNITS:
-                for t, half in complete_after(s - 2):
-                    multiply(t, half)
+                quantise(s - 1)
+                if s == 1:
+                    spread_bias()
+                add_bias(s - 1)
+            if 0 <= s - LAG < N_UNITS:
+                multiply(s - LAG)
             if s < N_UNITS and s % 2 == 1:
                 c_next = s // 2 + ATTN_BUFS
                 if c_next < N_CHUNKS:
                     load_chunk(c_next)
-            if 0 <= s - 3 < N_UNITS:
-                for t, half in complete_after(s - 3):
-                    add_product(t, half)
+            if 0 <= s - LAG - 1 < N_UNITS:
+                add_product(s - LAG - 1)
+                if (s - LAG - 1) % 2 == 1:
+                    store((s - LAG - 1) // 2)

from contextlib import ExitStack

import concourse.mybir as mybir
from concourse.masks import make_identity

F32 = mybir.dt.float32
BF16 = mybir.dt.bfloat16
U32 = mybir.dt.uint32
U8 = mybir.dt.uint8
FP8X4 = mybir.dt.float8_e4m3fn_x4
ADD = mybir.AluOpType.add

P = 128
FLOPS = 2 * 16384 * 512 * 128

N_CHUNKS = 16
N_UNITS = 2 * N_CHUNKS
ATTN_BUFS = 6
OUT_BUFS = 8
GPSIMD_BIAS_UNITS = ()
N_DUMMY = 2
LAG = 3


def tile_windowattentionblock_pb_t_kernel(tc, attn_ctx, x, wo, bo, out):
    nc = tc.nc
    attn_v = attn_ctx.rearrange("n (ti tj) h d -> (n ti) (tj h d)", tj=8)
    x_v = x.rearrange("b i (s r) c -> (b i s) (r c)", r=8)
    out_v = out.rearrange("b i (s r) c -> (b i s) (r c)", r=8)
    wo_v = wo.rearrange("h d c -> (h d) c").rearrange("(u q e) c -> q u (e c)", u=2, e=2)

    with ExitStack() as ctx:
        const = ctx.enter_context(tc.tile_pool(name="const", bufs=1))
        attn_pool = ctx.enter_context(tc.tile_pool(name="attn", bufs=ATTN_BUFS))
        grp_pool = ctx.enter_context(tc.tile_pool(name="grp", bufs=3))
        code_pool = ctx.enter_context(tc.tile_pool(name="code", bufs=5))
        out_pool = ctx.enter_context(tc.tile_pool(name="outp", bufs=OUT_BUFS))
        tp_pool = ctx.enter_context(tc.psum_pool(name="tp", bufs=4))
        mx_pool = ctx.enter_context(tc.psum_pool(name="mx", bufs=3))
        scr_pool = ctx.enter_context(tc.psum_pool(name="scr", bufs=1))
        ctx.enter_context(tc.manual_schedule())

        scratch = scr_pool.tile([P, 512], F32, name="scratch")
        attn_tiles = {}
        x_tiles = {}
        state = {}

        def slot_ranges(c):
            b, a = c // 4, c % 4
            if a < 3:
                return [(0, P, (b * 64 + 16 * a + 4) * 8)]
            return [(0, 96, (b * 64 + 52) * 8), (96, 32, b * 64 * 8)]

        def load_x(b, wrap):
            x_sb = x_tiles[b]
            if not wrap:
                s0 = (b * 64 + 4) * 8
                nc.sync.dma_start(
                    out=x_sb[:, 0:3, :],
                    in_=x_v[s0 : s0 + 3 * P, :].rearrange("(t q) f -> q t f", q=P),
                )
            else:
                for p0, n, s0 in slot_ranges(b * 4 + 3):
                    nc.sync.dma_start(out=x_sb[p0 : p0 + n, 3, :], in_=x_v[s0 : s0 + n, :])

        def load_attn(c, pieces=1):
            a_sb = attn_pool.tile([P, 4096], BF16, name="a_sb")
            w = 4096 // pieces
            for i in range(pieces):
                nc.sync.dma_start(
                    out=a_sb[:, i * w : (i + 1) * w],
                    in_=attn_v[c * P : (c + 1) * P, i * w : (i + 1) * w],
                )
                if c == 0 and i == 0:
                    nc.sync.dma_start(
                        out=w_raw[:].rearrange("p (u e) c -> p u (e c)", u=2), in_=wo_v
                    )
                    nc.sync.dma_start(out=brow[0:1, 0:P], in_=bo.unsqueeze(0))
            attn_tiles[c] = a_sb

        def load_chunk(c):
            if c > 0 and c % 4 == 0:
                load_x(c // 4, False)
            if c % 4 == 3:
                load_x(c // 4, True)
            load_attn(c)

        brow = const.tile([P, 256], BF16, name="brow")
        ones = const.tile([P, P], BF16, name="ones")
        nc.vector.memset(brow[:], 0.0)
        nc.vector.memset(ones[:], 1.0)
        ident = const.tile([P, P], F32, name="ident")
        make_identity(nc, ident[:])
        for b in range(4):
            x_tiles[b] = const.tile([P, 4, 1024], BF16, name="x_sb%d" % b)

        w_raw = const.tile([P, 4, P], BF16, name="w_raw")
        load_attn(0, pieces=2)
        load_x(0, False)
        for c in range(1, ATTN_BUFS):
            load_chunk(c)

        id_v = ident[:].rearrange("p (g j t) -> p g t j", g=2, j=8)
        perm_a = const.tile([P, 2, 8, 8], F32, name="perm_a")
        perm_b = const.tile([P, 2, 8, 8], F32, name="perm_b")
        nc.vector.tensor_copy(out=perm_a[:], in_=id_v)
        nc.vector.tensor_copy(out=perm_b[:, :, :, 1:8], in_=id_v[:, :, :, 0:7])
        nc.vector.tensor_copy(out=perm_b[:, :, :, 0:1], in_=id_v[:, :, :, 7:8])
        perms = [
            perm_a[:].rearrange("p g t s -> p (g t s)"),
            perm_b[:].rearrange("p g t s -> p (g t s)"),
        ]

        bias_bc = const.tile([P, P], F32, name="bias_bc")

        def spread_bias():
            bias_ps = mx_pool.tile([P, 4, P], F32, name="bias_ps", tag="mx")
            nc.tensor.matmul(
                out=bias_ps[:, 0:2, :].rearrange("p a c -> p (a c)"),
                lhsT=ones[:],
                rhs=brow[:],
                start=True,
                stop=True,
            )
            nc.vector.tensor_copy(out=bias_bc[:], in_=bias_ps[:, 0, :])

        w_grp = const.tile([P, P, 4], BF16, name="w_grp", align_bytes=64)
        nc.vector.tensor_copy(out=w_grp[:], in_=w_raw[:].rearrange("p t c -> p c t"))
        w_codes = const.tile([P, P], U32, name="w_codes", align_bytes=64)
        w_scales = const.tile([P, P], U8, name="w_scales", align_bytes=64)
        nc.vector.quantize_mx(
            out=w_codes[:].bitcast(FP8X4),
            scales=w_scales[:],
            in_=w_grp[:].rearrange("p c t -> p (c t)"),
        )

        def transpose_and_exit(u):
            a32 = attn_tiles[u // 2][:].bitcast(F32)
            grp = grp_pool.tile([P, 2048], BF16, name="grp", align_bytes=64)
            g32 = grp[:].bitcast(F32)
            banks = []
            for b in range(2):
                tp = tp_pool.tile([P, 2, 2, P], F32, name="tp")
                for a in range(2):
                    tj = (u % 2) * 4 + b * 2 + a
                    for h in range(2):
                        lo = tj * 256 + h * P
                        nc.tensor.transpose(tp[:, a, h, :], a32[:, lo : lo + P], perms[u % 2])
                banks.append(tp)
            for b in range(2):
                nc.scalar.copy(
                    out=g32[:, b * 512 : (b + 1) * 512].rearrange("p (a m h) -> p a m h", a=2, h=2),
                    in_=banks[b][:].rearrange("p a h m -> p a m h"),
                )
            state[("grp", u)] = grp

        def quantise(u):
            codes = code_pool.tile([P, 512], U32, name="codes", align_bytes=64)
            scales = code_pool.tile([P, 512], U8, name="scales", align_bytes=64)
            nc.vector.quantize_mx(
                out=codes[:].bitcast(FP8X4), scales=scales[:], in_=state[("grp", u)][:]
            )
            state[("codes", u)] = (codes, scales)

        def multiply(u):
            codes, scales = state[("codes", u)]
            mx = mx_pool.tile([P, 4, P], F32, name="mx")
            for a in range(4):
                cols = slice(a * P, (a + 1) * P)
                nc.tensor.matmul_mx(
                    out=mx[:, a, :],
                    lhsT=codes[:, cols].bitcast(FP8X4),
                    lhsT_scale=scales[:, cols],
                    rhs=w_codes[:].bitcast(FP8X4),
                    rhs_scale=w_scales[:],
                    start=True,
                    stop=True,
                )
            if u < N_UNITS - 3:
                for i in range(N_DUMMY):
                    nc.tensor.matmul_mx(
                        out=scratch[:],
                        lhsT=w_codes[:].bitcast(FP8X4),
                        lhsT_scale=w_scales[:],
                        rhs=codes[:].bitcast(FP8X4),
                        rhs_scale=scales[:],
                        start=True,
                        stop=True,
                    )
            state[("mx", u)] = mx

        def o_half(u):
            lo = 512 if u % 2 == 0 else 0
            return slice(lo, lo + 512)

        def add_bias(u):
            c = u // 2
            if u % 2 == 0:
                state[("o", c)] = out_pool.tile([P, 1024], F32, name="o_sb")
            eng = nc.gpsimd if u in GPSIMD_BIAS_UNITS else nc.vector
            eng.tensor_tensor(
                out=state[("o", c)][:, o_half(u)].rearrange("p (r c) -> p r c", r=4),
                in0=x_tiles[c // 4][:, c % 4, o_half(u)].rearrange("p (r c) -> p r c", r=4),
                in1=bias_bc[:].unsqueeze(1).to_broadcast([P, 4, P]),
                op=ADD,
            )

        def add_product(u):
            o_part = state[("o", u // 2)][:, o_half(u)]
            nc.vector.tensor_tensor(
                out=o_part,
                in0=state[("mx", u)][:].rearrange("p a c -> p (a c)"),
                in1=o_part,
                op=ADD,
            )

        def store(c):
            o_sb = state[("o", c)]
            for p0, n, s0 in slot_ranges(c):
                nc.sync.dma_start(out=out_v[s0 : s0 + n, :], in_=o_sb[p0 : p0 + n, :])

        for s in range(N_UNITS + LAG + 1):
            if s < N_UNITS:
                transpose_and_exit(s)
            if 0 <= s - 1 < N_UNITS:
                quantise(s - 1)
                if s == 1:
                    spread_bias()
                add_bias(s - 1)
            if 0 <= s - LAG < N_UNITS:
                multiply(s - LAG)
            if s < N_UNITS and s % 2 == 1:
                c_next = s // 2 + ATTN_BUFS
                if c_next < N_CHUNKS:
                    load_chunk(c_next)
            if 0 <= s - LAG - 1 < N_UNITS:
                add_product(s - LAG - 1)
                if (s - LAG - 1) % 2 == 1:
                    store((s - LAG - 1) // 2)
